import numpy as np
import ml_dtypes


def mxq(x, axis, fmt="e4m3"):
    dtype, down = {"e4m3": (ml_dtypes.float8_e4m3fn, 7), "e5m2": (ml_dtypes.float8_e5m2, 14)}[fmt]
    v = np.moveaxis(np.asarray(x, np.float32).astype(ml_dtypes.bfloat16).astype(np.float64), axis, -1)
    blocks = v.reshape(v.shape[:-1] + (-1, 32))
    amax = np.abs(blocks).max(-1, keepdims=True)
    byte = np.maximum(np.where(amax > 0, np.frexp(amax)[1] - 1 + 127, 0) - down, 1)
    scale = np.exp2(byte - 127.0)
    codes = (blocks / scale).astype(np.float32).astype(dtype).astype(np.float64)
    return np.moveaxis((codes * scale).reshape(v.shape), -1, axis)


WIDE = False


def mx_kscale(k):
    if not WIDE:
        return np.ones(k)
    levels = np.array([10, -10, 5, -5, 0])
    a = np.random.permutation(np.resize(levels, k // 512 * 4)).reshape(k // 512, 4)
    idx = np.arange(k)
    return np.exp2(a[idx // 512, idx % 128 // 32])


BF16 = ml_dtypes.bfloat16


def bf(x):
    return np.asarray(x, np.float32).astype(BF16)


def f64(x):
    return np.asarray(x).astype(np.float64)


B, N, C = 64, 16, 512
NEG_SLOPE = 0.2


def leaky(v):
    return np.where(v >= 0, v, NEG_SLOPE * v)


def setup_inputs():
    s, t = mx_kscale(C), mx_kscale(C)
    w1 = np.random.standard_normal((2, C, C)) * 0.7 / np.sqrt(C) / s[None, :, None] * t
    return {"F": bf(np.random.standard_normal((B, N, C)) * s),
            "W1": bf(w1.reshape(2 * C, C)),
            "b1": bf(np.random.standard_normal(C) * 0.2 * t),
            "W2": bf(np.random.standard_normal((C, C)) / np.sqrt(C) / t[:, None]),
            "b2": bf(np.random.standard_normal(C) * 0.2)}


def reference(F, W1, b1, W2, b2):
    Fq = mxq(f64(F), 2, "e4m3")
    W1 = f64(W1)
    A = Fq @ mxq(W1[:C], 0, "e4m3")
    Bp = Fq @ mxq(W1[C:], 0, "e4m3")
    h = leaky(A[:, :, None, :] + Bp[:, None, :, :] + f64(b1))
    h = leaky((mxq(h, 3, "e4m3") @ mxq(f64(W2), 0, "e4m3")) + f64(b2))
    return h.sum(-2)

@@ -1,0 +1,261 @@
+from contextlib import ExitStack
+
+import concourse.mybir as mybir
+from concourse.masks import make_identity
+
+FLOPS = 2 * 1024 * 1024 * 512 + 2 * 16384 * 512 * 512
+
+F32 = mybir.dt.float32
+BF16 = mybir.dt.bfloat16
+U32 = mybir.dt.uint32
+U8 = mybir.dt.uint8
+FP8X4 = mybir.dt.float8_e4m3fn_x4
+ALU = mybir.AluOpType
+ACT = mybir.ActivationFunctionType
+
+P = 128
+SETS = 64
+NODES = 16
+C = 512
+PACK = 4
+CHUNKS = 4
+WIN = 8
+COLS = WIN * SETS
+TILES = 32
+SLOPE = 0.2
+
+
+def tile_nonlocalmp_pa_t_kernel(tc, F, W1, b1, W2, b2, out):
+    nc = tc.nc
+    with ExitStack() as ctx:
+        ctx.enter_context(tc.manual_schedule())
+        const = ctx.enter_context(tc.tile_pool(name="const", bufs=1))
+        work = ctx.enter_context(tc.tile_pool(name="work", bufs=2))
+        psum = ctx.enter_context(tc.psum_pool(name="psum", bufs=2))
+
+        b1r = const.tile([P, CHUNKS], BF16, name="b1r", tag="b1r")
+        b2r = const.tile([P, CHUNKS], BF16, name="b2r", tag="b2r")
+        nc.scalar.dma_start(out=b1r[:], in_=b1.rearrange("(p t) -> p t", t=CHUNKS))
+        nc.scalar.dma_start(out=b2r[:], in_=b2.rearrange("(p t) -> p t", t=CHUNKS))
+
+        f_raw = const.tile([P, 8, C], BF16, name="f_raw", tag="f_raw")
+        f_rows = F.rearrange("b i c -> (b i) c").rearrange("(g p) c -> p g c", p=P)
+        nc.sync.dma_start(out=f_raw[:, 0:4, :], in_=f_rows[:, 0:4, :])
+        nc.sync.dma_start(out=f_raw[:, 4:8, :], in_=f_rows[:, 4:8, :])
+
+        w1_raw = const.tile([P, 2, PACK, C], BF16, name="w1_raw", tag="w1_raw")
+        for a in range(2):
+            for u in range(2):
+                r = a * C + u * 256
+                nc.sync.dma_start(
+                    out=w1_raw[:, a, 2 * u : 2 * u + 2, :],
+                    in_=W1[r : r + 256, :].rearrange("(p e) c -> p e c", e=2),
+                )
+        w2_raw = const.tile([P, PACK, C], BF16, name="w2_raw", tag="w2_raw")
+        nc.sync.dma_start(out=w2_raw[:], in_=W2.rearrange("(p t) n -> p t n", t=PACK))
+
+        ident = const.tile([P, P], F32, name="ident", tag="ident")
+        make_identity(nc, ident[:])
+
+        f_grp = const.tile([P, NODES, SETS, 2], F32, name="f_grp", tag="f_grp", align_bytes=64)
+        fc = const.tile([P, 2 * NODES * SETS], U32, name="fc", tag="fc", align_bytes=64)
+        fs = const.tile([P, 2 * NODES * SETS], U8, name="fs", tag="fs", align_bytes=64)
+        for gg in range(4):
+            xt = psum.tile([P, 2, 2, P], F32, name="xt", tag=("v" if gg % 2 == 0 else "x"))
+            for gp in range(2):
+                words = f_raw[:, 2 * gg + gp, :].bitcast(F32)
+                for u in range(2):
+                    nc.tensor.transpose(
+                        out=xt[:, u, gp, :], in_=words[:, P * u : P * u + P], identity=ident[:]
+                    )
+            dst = f_grp[:, :, 16 * gg : 16 * gg + 16, :]
+            src = xt[:].rearrange("p u g (b i) -> p i (g b) u", i=NODES)
+            if gg % 2 == 0:
+                nc.vector.tensor_copy(out=dst, in_=src)
+            else:
+                nc.scalar.copy(out=dst, in_=src)
+
+        w1_grp = const.tile([P, 2, CHUNKS, P, PACK], BF16, name="w1_grp", tag="w1_grp", align_bytes=64)
+        w1c = const.tile([P, 2 * C], U32, name="w1c", tag="w1c", align_bytes=64)
+        w1s = const.tile([P, 2 * C], U8, name="w1s", tag="w1s", align_bytes=64)
+        w2_grp = const.tile([P, CHUNKS, P, PACK], BF16, name="w2_grp", tag="w2_grp", align_bytes=64)
+        w2c = const.tile([P, C], U32, name="w2c", tag="w2c", align_bytes=64)
+        w2s = const.tile([P, C], U8, name="w2s", tag="w2s", align_bytes=64)
+
+        nc.vector.tensor_copy(
+            out=w1_grp[:, 0].rearrange("p o m t -> p m t o"),
+            in_=w1_raw[:, 0].rearrange("p t (m o) -> p m t o", o=CHUNKS),
+        )
+        nc.scalar.copy(
+            out=w1_grp[:, 1].rearrange("p o m t -> p m t o"),
+            in_=w1_raw[:, 1].rearrange("p t (m o) -> p m t o", o=CHUNKS),
+        )
+        f_bf = f_grp[:].rearrange("p i b u -> p (i b u)").bitcast(BF16)
+        nc.vector.quantize_mx(out=fc[:, 0:1024].bitcast(FP8X4), scales=fs[:, 0:1024], in_=f_bf)
+        for a in range(2):
+            nc.vector.quantize_mx(
+                out=w1c[:, a * C : (a + 1) * C].bitcast(FP8X4),
+                scales=w1s[:, a * C : (a + 1) * C],
+                in_=w1_grp[:, a].rearrange("p o m t -> p (o m t)"),
+            )
+        nc.scalar.copy(
+            out=w2_grp[:].rearrange("p o m t -> p m t o"),
+            in_=w2_raw[:].rearrange("p t (m o) -> p m t o", o=CHUNKS),
+        )
+
+        b1f = const.tile([P, CHUNKS], F32, name="b1f", tag="b1f")
+        nb2 = const.tile([P, CHUNKS], F32, name="nb2", tag="nb2")
+        b2x = const.tile([P, CHUNKS], F32, name="b2x", tag="b2x")
+        nc.vector.tensor_copy(out=b1f[:], in_=b1r[:])
+        nc.vector.tensor_scalar(out=nb2[:], in0=b2r[:], scalar1=-1.0, scalar2=None, op0=ALU.mult)
+        nc.vector.tensor_scalar(out=b2x[:], in0=b2r[:], scalar1=20.0, scalar2=None, op0=ALU.mult)
+
+        acc = [
+            [const.tile([P, COLS], F32, name="acc%d%d" % (h, m), tag="acc%d%d" % (h, m)) for m in range(CHUNKS)]
+            for h in range(2)
+        ]
+        tmp = [
+            [const.tile([P, COLS], F32, name="tmp%d%d" % (h, m), tag="tmp%d%d" % (h, m)) for m in range(CHUNKS)]
+            for h in range(2)
+        ]
+
+        def mx(dst, lw, ls, rw, rs, start, stop):
+            nc.tensor.matmul_mx(
+                out=dst,
+                lhsT=lw.bitcast(FP8X4),
+                lhsT_scale=ls,
+                rhs=rw.bitcast(FP8X4),
+                rhs_scale=rs,
+                start=start,
+                stop=stop,
+            )
+
+        p_tiles = {}
+        h_tiles = {}
+        code_tiles = {}
+        lin = {}
+
+        def emit_v(n, t):
+            if n >= TILES:
+                return
+            if t == 0:
+                p_tiles[n] = work.tile([P, CHUNKS, COLS], F32, name="pre", tag="pre", bufs=3)
+            r0 = WIN * (n // NODES)
+            a0 = SETS * r0
+            b0 = SETS * (r0 + n % NODES)
+            vt = psum.tile([P, COLS], F32, name="vt", tag="v")
+            wa = slice(t * P, (t + 1) * P)
+            wb = slice(C + t * P, C + (t + 1) * P)
+            mx(vt[:], w1c[:, wa], w1s[:, wa], fc[:, a0 : a0 + COLS], fs[:, a0 : a0 + COLS], True, False)
+            mx(vt[:], w1c[:, wb], w1s[:, wb], fc[:, b0 : b0 + COLS], fs[:, b0 : b0 + COLS], False, True)
+            nc.scalar.activation(
+                out=p_tiles[n][:, t, :], in_=vt[:], func=ACT.Identity, bias=b1f[:, t : t + 1], scale=1.0
+            )
+
+        def emit_h(n):
+            if n >= TILES:
+                return
+            ht = work.tile([P, COLS, PACK], BF16, name="hid", tag="hid", bufs=2, align_bytes=64)
+            h_tiles[n] = ht
+            pv = p_tiles[n][:].rearrange("p t w -> p w t")
+            nc.vector.scalar_tensor_tensor(
+                out=ht[:], in0=pv, scalar=SLOPE, in1=pv, op0=ALU.mult, op1=ALU.max
+            )
+
+        def emit_q(n):
+            if n >= TILES:
+                return
+            hc = work.tile([P, COLS], U32, name="hc", tag="hc", bufs=3, align_bytes=64)
+            hs = work.tile([P, COLS], U8, name="hs", tag="hs", bufs=3, align_bytes=64)
+            code_tiles[n] = (hc, hs)
+            nc.vector.quantize_mx(
+                out=hc[:].bitcast(FP8X4), scales=hs[:], in_=h_tiles[n][:].rearrange("p w t -> p (w t)")
+            )
+
+        def emit_x(n, m):
+            hc, hs = code_tiles[n]
+            xt2 = psum.tile([P, COLS], F32, name="xs", tag="x")
+            wm = slice(m * P, (m + 1) * P)
+            mx(xt2[:], w2c[:, wm], w2s[:, wm], hc[:], hs[:], True, True)
+            return xt2
+
+        def emit_l(n, m):
+            hc, hs = code_tiles[n]
+            s = n % NODES
+            if s == 0:
+                lin[m] = psum.tile([P, COLS], F32, name="lin%d" % m, tag="lin%d" % m, bufs=1)
+            wm = slice(m * P, (m + 1) * P)
+            mx(lin[m][:], w2c[:, wm], w2s[:, wm], hc[:], hs[:], s == 0, s == NODES - 1)
+
+        def emit_g(n, m, xt2):
+            a = acc[n // NODES][m]
+            if n % NODES == 0:
+                nc.vector.tensor_scalar(
+                    out=a[:], in0=xt2[:], scalar1=nb2[:, m : m + 1], scalar2=b2x[:, m : m + 1],
+                    op0=ALU.max, op1=ALU.add,
+                )
+            else:
+                nc.vector.scalar_tensor_tensor(
+                    out=a[:], in0=xt2[:], scalar=nb2[:, m : m + 1], in1=a[:], op0=ALU.max, op1=ALU.add
+                )
+
+        def emit_tmp(h):
+            for m in range(CHUNKS):
+                nc.vector.scalar_tensor_tensor(
+                    out=tmp[h][m][:], in0=lin[m][:], scalar=0.25, in1=acc[h][m][:], op0=ALU.mult, op1=ALU.add
+                )
+
+        def emit_out(h, q, tag, on_vector):
+            tp = psum.tile([P, CHUNKS, P], F32, name="tp", tag=tag)
+            for m in range(CHUNKS):
+                nc.tensor.transpose(out=tp[:, m, :], in_=tmp[h][m][:, q * P : (q + 1) * P], identity=ident[:])
+            res = work.tile([P, P, CHUNKS], F32, name="res", tag="res", bufs=4)
+            src = tp[:].rearrange("p m c -> p c m")
+            if on_vector:
+                nc.vector.tensor_scalar(out=res[:], in0=src, scalar1=0.8, scalar2=None, op0=ALU.mult)
+            else:
+                nc.scalar.mul(out=res[:], in_=src, mul=0.8)
+            for k in range(2):
+                node = WIN * h + 2 * q + k
+                nc.sync.dma_start(
+                    out=out[:, node, :], in_=res[k * SETS : (k + 1) * SETS].rearrange("p c m -> p (c m)")
+                )
+
+        for t in range(CHUNKS):
+            emit_v(0, t)
+        nc.vector.quantize_mx(
+            out=w2c[:].bitcast(FP8X4), scales=w2s[:], in_=w2_grp[:].rearrange("p o m t -> p (o m t)")
+        )
+        emit_h(0)
+        for t in range(CHUNKS):
+            emit_v(1, t)
+        nc.vector.quantize_mx(out=fc[:, 1024:2048].bitcast(FP8X4), scales=fs[:, 1024:2048], in_=f_bf)
+        emit_q(0)
+
+        for n in range(TILES):
+            emit_h(n + 1)
+            x0 = emit_x(n, 0)
+            x1 = emit_x(n, 1)
+            emit_v(n + 2, 0)
+            emit_v(n + 2, 1)
+            emit_g(n, 0, x0)
+            emit_g(n, 1, x1)
+            emit_l(n, 0)
+            emit_l(n, 1)
+            emit_v(n + 2, 2)
+            emit_q(n + 1)
+            x2 = emit_x(n, 2)
+            emit_v(n + 2, 3)
+            x3 = emit_x(n, 3)
+            emit_g(n, 2, x2)
+            emit_g(n, 3, x3)
+            emit_l(n, 2)
+            emit_l(n, 3)
+            if n == NODES - 1:
+                emit_tmp(0)
+            if NODES <= n < NODES + 4:
+                emit_out(0, n - NODES, "v", False)
+
+        emit_tmp(1)
+        for q in range(4):
+            emit_out(1, q, "v" if q % 2 == 0 else "x", q % 2 == 1)

@@ -38,11 +38,6 @@ def tile_nonlocalmp_pa_t_kernel(tc, F, W1, b1, W2, b2, out):
         nc.scalar.dma_start(out=b1r[:], in_=b1.rearrange("(p t) -> p t", t=CHUNKS))
         nc.scalar.dma_start(out=b2r[:], in_=b2.rearrange("(p t) -> p t", t=CHUNKS))
 
-        f_raw = const.tile([P, 8, C], BF16, name="f_raw", tag="f_raw")
-        f_rows = F.rearrange("b i c -> (b i) c").rearrange("(g p) c -> p g c", p=P)
-        nc.sync.dma_start(out=f_raw[:, 0:4, :], in_=f_rows[:, 0:4, :])
-        nc.sync.dma_start(out=f_raw[:, 4:8, :], in_=f_rows[:, 4:8, :])
-
         w1_raw = const.tile([P, 2, PACK, C], BF16, name="w1_raw", tag="w1_raw")
         for a in range(2):
             for u in range(2):
@@ -51,6 +46,10 @@ def tile_nonlocalmp_pa_t_kernel(tc, F, W1, b1, W2, b2, out):
                     out=w1_raw[:, a, 2 * u : 2 * u + 2, :],
                     in_=W1[r : r + 256, :].rearrange("(p e) c -> p e c", e=2),
                 )
+        f_raw = const.tile([P, 8, C], BF16, name="f_raw", tag="f_raw")
+        f_rows = F.rearrange("b i c -> (b i) c").rearrange("(g p) c -> p g c", p=P)
+        nc.sync.dma_start(out=f_raw[:, 0:4, :], in_=f_rows[:, 0:4, :])
+        nc.sync.dma_start(out=f_raw[:, 4:8, :], in_=f_rows[:, 4:8, :])
         w2_raw = const.tile([P, PACK, C], BF16, name="w2_raw", tag="w2_raw")
         nc.sync.dma_start(out=w2_raw[:], in_=W2.rearrange("(p t) n -> p t n", t=PACK))
 
@@ -70,10 +69,7 @@ def tile_nonlocalmp_pa_t_kernel(tc, F, W1, b1, W2, b2, out):
                     )
             dst = f_grp[:, :, 16 * gg : 16 * gg + 16, :]
             src = xt[:].rearrange("p u g (b i) -> p i (g b) u", i=NODES)
-            if gg % 2 == 0:
-                nc.vector.tensor_copy(out=dst, in_=src)
-            else:
-                nc.scalar.copy(out=dst, in_=src)
+            nc.scalar.copy(out=dst, in_=src)
 
         w1_grp = const.tile([P, 2, CHUNKS, P, PACK], BF16, name="w1_grp", tag="w1_grp", align_bytes=64)
         w1c = const.tile([P, 2 * C], U32, name="w1c", tag="w1c", align_bytes=64)
@@ -86,22 +82,16 @@ def tile_nonlocalmp_pa_t_kernel(tc, F, W1, b1, W2, b2, out):
             out=w1_grp[:, 0].rearrange("p o m t -> p m t o"),
             in_=w1_raw[:, 0].rearrange("p t (m o) -> p m t o", o=CHUNKS),
         )
-        nc.scalar.copy(
+        nc.vector.tensor_copy(
             out=w1_grp[:, 1].rearrange("p o m t -> p m t o"),
             in_=w1_raw[:, 1].rearrange("p t (m o) -> p m t o", o=CHUNKS),
         )
-        f_bf = f_grp[:].rearrange("p i b u -> p (i b u)").bitcast(BF16)
-        nc.vector.quantize_mx(out=fc[:, 0:1024].bitcast(FP8X4), scales=fs[:, 0:1024], in_=f_bf)
         for a in range(2):
             nc.vector.quantize_mx(
                 out=w1c[:, a * C : (a + 1) * C].bitcast(FP8X4),
                 scales=w1s[:, a * C : (a + 1) * C],
                 in_=w1_grp[:, a].rearrange("p o m t -> p (o m t)"),
             )
-        nc.scalar.copy(
-            out=w2_grp[:].rearrange("p o m t -> p m t o"),
-            in_=w2_raw[:].rearrange("p t (m o) -> p m t o", o=CHUNKS),
-        )
 
         b1f = const.tile([P, CHUNKS], F32, name="b1f", tag="b1f")
         nb2 = const.tile([P, CHUNKS], F32, name="nb2", tag="nb2")
@@ -109,6 +99,10 @@ def tile_nonlocalmp_pa_t_kernel(tc, F, W1, b1, W2, b2, out):
         nc.vector.tensor_copy(out=b1f[:], in_=b1r[:])
         nc.vector.tensor_scalar(out=nb2[:], in0=b2r[:], scalar1=-1.0, scalar2=None, op0=ALU.mult)
         nc.vector.tensor_scalar(out=b2x[:], in0=b2r[:], scalar1=20.0, scalar2=None, op0=ALU.mult)
+        b1s = const.tile([P, CHUNKS], F32, name="b1s", tag="b1s")
+        nc.vector.tensor_scalar(out=b1s[:], in0=b1r[:], scalar1=SLOPE, scalar2=None, op0=ALU.mult)
+        f_bf = f_grp[:].rearrange("p i b u -> p (i b u)").bitcast(BF16)
+        nc.vector.quantize_mx(out=fc[:, 0:1024].bitcast(FP8X4), scales=fs[:, 0:1024], in_=f_bf)
 
         acc = [
             [const.tile([P, COLS], F32, name="acc%d%d" % (h, m), tag="acc%d%d" % (h, m)) for m in range(CHUNKS)]
@@ -139,7 +133,7 @@ def tile_nonlocalmp_pa_t_kernel(tc, F, W1, b1, W2, b2, out):
             if n >= TILES:
                 return
             if t == 0:
-                p_tiles[n] = work.tile([P, CHUNKS, COLS], F32, name="pre", tag="pre", bufs=3)
+                p_tiles[n] = work.tile([P, 2, CHUNKS, COLS], BF16, name="pre", tag="pre", bufs=3)
             r0 = WIN * (n // NODES)
             a0 = SETS * r0
             b0 = SETS * (r0 + n % NODES)
@@ -148,18 +142,36 @@ def tile_nonlocalmp_pa_t_kernel(tc, F, W1, b1, W2, b2, out):
             wb = slice(C + t * P, C + (t + 1) * P)
             mx(vt[:], w1c[:, wa], w1s[:, wa], fc[:, a0 : a0 + COLS], fs[:, a0 : a0 + COLS], True, False)
             mx(vt[:], w1c[:, wb], w1s[:, wb], fc[:, b0 : b0 + COLS], fs[:, b0 : b0 + COLS], False, True)
-            nc.scalar.activation(
-                out=p_tiles[n][:, t, :], in_=vt[:], func=ACT.Identity, bias=b1f[:, t : t + 1], scale=1.0
-            )
+            if n == 0 and t % 2 == 1:
+                nc.vector.tensor_scalar(
+                    out=p_tiles[n][:, 0, t, :], in0=vt[:], scalar1=b1f[:, t : t + 1], scalar2=None, op0=ALU.add
+                )
+                nc.vector.tensor_scalar(
+                    out=p_tiles[n][:, 1, t, :], in0=vt[:], scalar1=b1f[:, t : t + 1], scalar2=SLOPE,
+                    op0=ALU.add, op1=ALU.mult,
+                )
+            else:
+                nc.scalar.activation(
+                    out=p_tiles[n][:, 0, t, :], in_=vt[:], func=ACT.Identity, bias=b1f[:, t : t + 1], scale=1.0
+                )
+                nc.scalar.activation(
+                    out=p_tiles[n][:, 1, t, :], in_=vt[:], func=ACT.Identity, bias=b1s[:, t : t + 1], scale=SLOPE
+                )
 
-        def emit_h(n):
+        def emit_m(n):
+            if n >= TILES:
+                return
+            pq = p_tiles[n]
+            nc.vector.tensor_tensor(out=pq[:, 0], in0=pq[:, 0], in1=pq[:, 1], op=ALU.max)
+
+        def emit_r(n):
             if n >= TILES:
                 return
             ht = work.tile([P, COLS, PACK], BF16, name="hid", tag="hid", bufs=2, align_bytes=64)
             h_tiles[n] = ht
-            pv = p_tiles[n][:].rearrange("p t w -> p w t")
-            nc.vector.scalar_tensor_tensor(
-                out=ht[:], in0=pv, scalar=SLOPE, in1=pv, op0=ALU.mult, op1=ALU.max
+            nc.vector.tensor_copy(
+                out=ht[:].rearrange("p (c i) t -> p c t i", i=4),
+                in_=p_tiles[n][:, 0].rearrange("p t (c i) -> p c t i", i=4),
             )
 
         def emit_q(n):
@@ -223,34 +235,40 @@ def tile_nonlocalmp_pa_t_kernel(tc, F, W1, b1, W2, b2, out):
 
         for t in range(CHUNKS):
             emit_v(0, t)
+        nc.vector.tensor_copy(
+            out=w2_grp[:].rearrange("p o m t -> p m t o"),
+            in_=w2_raw[:].rearrange("p t (m o) -> p m t o", o=CHUNKS),
+        )
+        emit_m(0)
         nc.vector.quantize_mx(
             out=w2c[:].bitcast(FP8X4), scales=w2s[:], in_=w2_grp[:].rearrange("p o m t -> p (o m t)")
         )
-        emit_h(0)
+        emit_r(0)
         for t in range(CHUNKS):
             emit_v(1, t)
         nc.vector.quantize_mx(out=fc[:, 1024:2048].bitcast(FP8X4), scales=fs[:, 1024:2048], in_=f_bf)
         emit_q(0)
 
         for n in range(TILES):
-            emit_h(n + 1)
+            emit_m(n + 1)
             x0 = emit_x(n, 0)
-            x1 = emit_x(n, 1)
             emit_v(n + 2, 0)
-            emit_v(n + 2, 1)
+            x1 = emit_x(n, 1)
             emit_g(n, 0, x0)
-            emit_g(n, 1, x1)
             emit_l(n, 0)
             emit_l(n, 1)
+            emit_v(n + 2, 1)
+            emit_r(n + 1)
+            emit_g(n, 1, x1)
+            x2 = emit_x(n, 2)
+            emit_l(n, 2)
             emit_v(n + 2, 2)
             emit_q(n + 1)
-            x2 = emit_x(n, 2)
-            emit_v(n + 2, 3)
-            x3 = emit_x(n, 3)
             emit_g(n, 2, x2)
-            emit_g(n, 3, x3)
-            emit_l(n, 2)
+            x3 = emit_x(n, 3)
             emit_l(n, 3)
+            emit_v(n + 2, 3)
+            emit_g(n, 3, x3)
             if n == NODES - 1:
                 emit_tmp(0)
             if NODES <= n < NODES + 4:

@@ -23,6 +23,8 @@ WIN = 8
 COLS = WIN * SETS
 TILES = 32
 SLOPE = 0.2
+GW = 160
+AHEAD = 4
 
 
 def tile_nonlocalmp_pa_t_kernel(tc, F, W1, b1, W2, b2, out):
@@ -133,7 +135,7 @@ def tile_nonlocalmp_pa_t_kernel(tc, F, W1, b1, W2, b2, out):
             if n >= TILES:
                 return
             if t == 0:
-                p_tiles[n] = work.tile([P, 2, CHUNKS, COLS], BF16, name="pre", tag="pre", bufs=3)
+                p_tiles[n] = work.tile([P, 2, CHUNKS, COLS], BF16, name="pre", tag="pre", bufs=5)
             r0 = WIN * (n // NODES)
             a0 = SETS * r0
             b0 = SETS * (r0 + n % NODES)
@@ -142,7 +144,7 @@ def tile_nonlocalmp_pa_t_kernel(tc, F, W1, b1, W2, b2, out):
             wb = slice(C + t * P, C + (t + 1) * P)
             mx(vt[:], w1c[:, wa], w1s[:, wa], fc[:, a0 : a0 + COLS], fs[:, a0 : a0 + COLS], True, False)
             mx(vt[:], w1c[:, wb], w1s[:, wb], fc[:, b0 : b0 + COLS], fs[:, b0 : b0 + COLS], False, True)
-            if n == 0 and t % 2 == 1:
+            if n < 2 and t % 2 == 1:
                 nc.vector.tensor_scalar(
                     out=p_tiles[n][:, 0, t, :], in0=vt[:], scalar1=b1f[:, t : t + 1], scalar2=None, op0=ALU.add
                 )
@@ -161,21 +163,29 @@ def tile_nonlocalmp_pa_t_kernel(tc, F, W1, b1, W2, b2, out):
         def emit_m(n):
             if n >= TILES:
                 return
+            h_tiles[n] = work.tile([P, COLS, PACK], BF16, name="hid", tag="hid", bufs=3, align_bytes=64)
             pq = p_tiles[n]
             nc.vector.tensor_tensor(out=pq[:, 0], in0=pq[:, 0], in1=pq[:, 1], op=ALU.max)
 
         def emit_r(n):
             if n >= TILES:
                 return
-            ht = work.tile([P, COLS, PACK], BF16, name="hid", tag="hid", bufs=2, align_bytes=64)
-            h_tiles[n] = ht
             nc.vector.tensor_copy(
-                out=ht[:].rearrange("p (c i) t -> p c t i", i=4),
-                in_=p_tiles[n][:, 0].rearrange("p t (c i) -> p c t i", i=4),
+                out=h_tiles[n][:, 0 : COLS - GW, :].rearrange("p (c i) t -> p c t i", i=4),
+                in_=p_tiles[n][:, 0, :, 0 : COLS - GW].rearrange("p t (c i) -> p c t i", i=4),
+            )
+
+        def emit_rg(n):
+            if n >= TILES or GW == 0:
+                return
+            nc.gpsimd.tensor_scalar(
+                out=h_tiles[n][:, COLS - GW : COLS, :],
+                in0=p_tiles[n][:, 0, :, COLS - GW : COLS].rearrange("p t w -> p w t"),
+                scalar1=1.0, scalar2=0.0, op0=ALU.mult, op1=ALU.add,
             )
 
         def emit_q(n):
-            if n >= TILES:
+            if n >= TILES or n < 0:
                 return
             hc = work.tile([P, COLS], U32, name="hc", tag="hc", bufs=3, align_bytes=64)
             hs = work.tile([P, COLS], U8, name="hs", tag="hs", bufs=3, align_bytes=64)
@@ -239,36 +249,42 @@ def tile_nonlocalmp_pa_t_kernel(tc, F, W1, b1, W2, b2, out):
             out=w2_grp[:].rearrange("p o m t -> p m t o"),
             in_=w2_raw[:].rearrange("p t (m o) -> p m t o", o=CHUNKS),
         )
-        emit_m(0)
+        for t in range(CHUNKS):
+            emit_v(1, t)
         nc.vector.quantize_mx(
             out=w2c[:].bitcast(FP8X4), scales=w2s[:], in_=w2_grp[:].rearrange("p o m t -> p (o m t)")
         )
-        emit_r(0)
-        for t in range(CHUNKS):
-            emit_v(1, t)
-        nc.vector.quantize_mx(out=fc[:, 1024:2048].bitcast(FP8X4), scales=fs[:, 1024:2048], in_=f_bf)
-        emit_q(0)
 
-        for n in range(TILES):
-            emit_m(n + 1)
-            x0 = emit_x(n, 0)
-            emit_v(n + 2, 0)
-            x1 = emit_x(n, 1)
-            emit_g(n, 0, x0)
-            emit_l(n, 0)
-            emit_l(n, 1)
-            emit_v(n + 2, 1)
-            emit_r(n + 1)
-            emit_g(n, 1, x1)
-            x2 = emit_x(n, 2)
-            emit_l(n, 2)
-            emit_v(n + 2, 2)
+        for n in range(-2, TILES):
+            live = n >= 0
+            emit_m(n + 2)
+            emit_rg(n + 2)
+            if live:
+                x0 = emit_x(n, 0)
+                x1 = emit_x(n, 1)
+            emit_v(n + AHEAD, 0)
+            if live:
+                emit_g(n, 0, x0)
+                emit_l(n, 0)
+                x2 = emit_x(n, 2)
+                emit_g(n, 1, x1)
+            emit_r(n + 2)
+            if n == -2:
+                nc.vector.quantize_mx(out=fc[:, 1024:2048].bitcast(FP8X4), scales=fs[:, 1024:2048], in_=f_bf)
             emit_q(n + 1)
-            emit_g(n, 2, x2)
-            x3 = emit_x(n, 3)
-            emit_l(n, 3)
-            emit_v(n + 2, 3)
-            emit_g(n, 3, x3)
+            if live:
+                emit_l(n, 1)
+            emit_v(n + AHEAD, 1)
+            if live:
+                x3 = emit_x(n, 3)
+                emit_g(n, 2, x2)
+                emit_l(n, 2)
+            emit_v(n + AHEAD, 2)
+            if live:
+                emit_l(n, 3)
+            emit_v(n + AHEAD, 3)
+            if live:
+                emit_g(n, 3, x3)
             if n == NODES - 1:
                 emit_tmp(0)
             if NODES <= n < NODES + 4:

@@ -25,6 +25,7 @@ TILES = 32
 SLOPE = 0.2
 GW = 160
 AHEAD = 4
+LATE = [(0, 4), (5, 9), (10, 14), (15, 15)]
 
 
 def tile_nonlocalmp_pa_t_kernel(tc, F, W1, b1, W2, b2, out):
@@ -62,7 +63,7 @@ def tile_nonlocalmp_pa_t_kernel(tc, F, W1, b1, W2, b2, out):
         fc = const.tile([P, 2 * NODES * SETS], U32, name="fc", tag="fc", align_bytes=64)
         fs = const.tile([P, 2 * NODES * SETS], U8, name="fs", tag="fs", align_bytes=64)
         for gg in range(4):
-            xt = psum.tile([P, 2, 2, P], F32, name="xt", tag=("v" if gg % 2 == 0 else "x"))
+            xt = psum.tile([P, 2, 2, P], F32, name="xt", tag="v", bufs=3)
             for gp in range(2):
                 words = f_raw[:, 2 * gg + gp, :].bitcast(F32)
                 for u in range(2):
@@ -110,10 +111,7 @@ def tile_nonlocalmp_pa_t_kernel(tc, F, W1, b1, W2, b2, out):
             [const.tile([P, COLS], F32, name="acc%d%d" % (h, m), tag="acc%d%d" % (h, m)) for m in range(CHUNKS)]
             for h in range(2)
         ]
-        tmp = [
-            [const.tile([P, COLS], F32, name="tmp%d%d" % (h, m), tag="tmp%d%d" % (h, m)) for m in range(CHUNKS)]
-            for h in range(2)
-        ]
+        tmp = acc
 
         def mx(dst, lw, ls, rw, rs, start, stop):
             nc.tensor.matmul_mx(
@@ -139,7 +137,7 @@ def tile_nonlocalmp_pa_t_kernel(tc, F, W1, b1, W2, b2, out):
             r0 = WIN * (n // NODES)
             a0 = SETS * r0
             b0 = SETS * (r0 + n % NODES)
-            vt = psum.tile([P, COLS], F32, name="vt", tag="v")
+            vt = psum.tile([P, COLS], F32, name="vt", tag="v", bufs=3)
             wa = slice(t * P, (t + 1) * P)
             wb = slice(C + t * P, C + (t + 1) * P)
             mx(vt[:], w1c[:, wa], w1s[:, wa], fc[:, a0 : a0 + COLS], fs[:, a0 : a0 + COLS], True, False)
@@ -187,8 +185,8 @@ def tile_nonlocalmp_pa_t_kernel(tc, F, W1, b1, W2, b2, out):
         def emit_q(n):
             if n >= TILES or n < 0:
                 return
-            hc = work.tile([P, COLS], U32, name="hc", tag="hc", bufs=3, align_bytes=64)
-            hs = work.tile([P, COLS], U8, name="hs", tag="hs", bufs=3, align_bytes=64)
+            hc = const.tile([P, COLS], U32, name="hc%d" % n, tag="hc%d" % n, align_bytes=64)
+            hs = const.tile([P, COLS], U8, name="hs%d" % n, tag="hs%d" % n, align_bytes=64)
             code_tiles[n] = (hc, hs)
             nc.vector.quantize_mx(
                 out=hc[:].bitcast(FP8X4), scales=hs[:], in_=h_tiles[n][:].rearrange("p w t -> p (w t)")
@@ -209,6 +207,16 @@ def tile_nonlocalmp_pa_t_kernel(tc, F, W1, b1, W2, b2, out):
             wm = slice(m * P, (m + 1) * P)
             mx(lin[m][:], w2c[:, wm], w2s[:, wm], hc[:], hs[:], s == 0, s == NODES - 1)
 
+        def emit_late(h, first, last):
+            m = CHUNKS - 1
+            wm = slice(m * P, (m + 1) * P)
+            for n in range(NODES * h + first, NODES * h + last + 1):
+                s = n % NODES
+                if s == 0:
+                    lin[m] = psum.tile([P, COLS], F32, name="lin3", tag="v", bufs=3)
+                hc, hs = code_tiles[n]
+                mx(lin[m][:], w2c[:, wm], w2s[:, wm], hc[:], hs[:], s == 0, s == NODES - 1)
+
         def emit_g(n, m, xt2):
             a = acc[n // NODES][m]
             if n % NODES == 0:
@@ -221,14 +229,14 @@ def tile_nonlocalmp_pa_t_kernel(tc, F, W1, b1, W2, b2, out):
                     out=a[:], in0=xt2[:], scalar=nb2[:, m : m + 1], in1=a[:], op0=ALU.max, op1=ALU.add
                 )
 
-        def emit_tmp(h):
-            for m in range(CHUNKS):
+        def emit_tmp(h, chunks):
+            for m in chunks:
                 nc.vector.scalar_tensor_tensor(
                     out=tmp[h][m][:], in0=lin[m][:], scalar=0.25, in1=acc[h][m][:], op0=ALU.mult, op1=ALU.add
                 )
 
         def emit_out(h, q, tag, on_vector):
-            tp = psum.tile([P, CHUNKS, P], F32, name="tp", tag=tag)
+            tp = psum.tile([P, CHUNKS, P], F32, name="tp", tag=tag, bufs=(3 if tag == "v" else 2))
             for m in range(CHUNKS):
                 nc.tensor.transpose(out=tp[:, m, :], in_=tmp[h][m][:, q * P : (q + 1) * P], identity=ident[:])
             res = work.tile([P, P, CHUNKS], F32, name="res", tag="res", bufs=4)
@@ -272,24 +280,28 @@ def tile_nonlocalmp_pa_t_kernel(tc, F, W1, b1, W2, b2, out):
             if n == -2:
                 nc.vector.quantize_mx(out=fc[:, 1024:2048].bitcast(FP8X4), scales=fs[:, 1024:2048], in_=f_bf)
             emit_q(n + 1)
-            if live:
-                emit_l(n, 1)
             emit_v(n + AHEAD, 1)
             if live:
                 x3 = emit_x(n, 3)
                 emit_g(n, 2, x2)
-                emit_l(n, 2)
+                emit_l(n, 1)
             emit_v(n + AHEAD, 2)
             if live:
-                emit_l(n, 3)
+                emit_l(n, 2)
+            if NODES <= n < NODES + 8:
+                emit_late(0, 2 * (n - NODES), 2 * (n - NODES) + 1)
+            if n >= TILES - 4:
+                emit_late(1, LATE[n - TILES + 4][0], LATE[n - TILES + 4][1])
             emit_v(n + AHEAD, 3)
             if live:
                 emit_g(n, 3, x3)
             if n == NODES - 1:
-                emit_tmp(0)
-            if NODES <= n < NODES + 4:
-                emit_out(0, n - NODES, "v", False)
+                emit_tmp(0, [0, 1, 2])
+            if n == NODES + 7:
+                emit_tmp(0, [3])
+            if NODES + 8 <= n < NODES + 12:
+                emit_out(0, n - NODES - 8, "v", False)
 
-        emit_tmp(1)
+        emit_tmp(1, [0, 1, 2, 3])
         for q in range(4):
             emit_out(1, q, "v" if q % 2 == 0 else "x", q % 2 == 1)

@@ -23,7 +23,7 @@ WIN = 8
 COLS = WIN * SETS
 TILES = 32
 SLOPE = 0.2
-GW = 160
+GW = 320
 AHEAD = 4
 LATE = [(0, 4), (5, 9), (10, 14), (15, 15)]
 
@@ -105,7 +105,12 @@ def tile_nonlocalmp_pa_t_kernel(tc, F, W1, b1, W2, b2, out):
         b1s = const.tile([P, CHUNKS], F32, name="b1s", tag="b1s")
         nc.vector.tensor_scalar(out=b1s[:], in0=b1r[:], scalar1=SLOPE, scalar2=None, op0=ALU.mult)
         f_bf = f_grp[:].rearrange("p i b u -> p (i b u)").bitcast(BF16)
-        nc.vector.quantize_mx(out=fc[:, 0:1024].bitcast(FP8X4), scales=fs[:, 0:1024], in_=f_bf)
+        for hf in range(2):
+            nc.vector.quantize_mx(
+                out=fc[:, hf * COLS : (hf + 1) * COLS].bitcast(FP8X4),
+                scales=fs[:, hf * COLS : (hf + 1) * COLS],
+                in_=f_bf[:, hf * COLS * PACK : (hf + 1) * COLS * PACK],
+            )
 
         acc = [
             [const.tile([P, COLS], F32, name="acc%d%d" % (h, m), tag="acc%d%d" % (h, m)) for m in range(CHUNKS)]
@@ -302,6 +307,24 @@ def tile_nonlocalmp_pa_t_kernel(tc, F, W1, b1, W2, b2, out):
             if NODES + 8 <= n < NODES + 12:
                 emit_out(0, n - NODES - 8, "v", False)
 
-        emit_tmp(1, [0, 1, 2, 3])
+        tps = []
         for q in range(4):
-            emit_out(1, q, "v" if q % 2 == 0 else "x", q % 2 == 1)
+            tag = "v" if q < 2 else "x"
+            tps.append(psum.tile([P, CHUNKS, P], F32, name="tq%d" % q, tag=tag, bufs=(3 if tag == "v" else 2)))
+        for m in range(CHUNKS):
+            emit_tmp(1, [m])
+            for q in range(4):
+                nc.tensor.transpose(out=tps[q][:, m, :], in_=tmp[1][m][:, q * P : (q + 1) * P], identity=ident[:])
+        for q in range(4):
+            res = work.tile([P, P, CHUNKS], F32, name="res", tag="res", bufs=4)
+            src = tps[q][:].rearrange("p m c -> p c m")
+            if q % 2 == 1:
+                nc.vector.tensor_scalar(out=res[:], in0=src, scalar1=0.8, scalar2=None, op0=ALU.mult)
+            else:
+                nc.scalar.mul(out=res[:], in_=src, mul=0.8)
+            for k in range(2):
+                node = WIN + 2 * q + k
+                eng = nc.sync if k == 0 else nc.scalar
+                eng.dma_start(
+                    out=out[:, node, :], in_=res[k * SETS : (k + 1) * SETS].rearrange("p c m -> p (c m)")
+                )

@@ -23,7 +23,8 @@ WIN = 8
 COLS = WIN * SETS
 TILES = 32
 SLOPE = 0.2
-GW = 320
+VS = 96
+HALF = 256
 AHEAD = 4
 LATE = [(0, 4), (5, 9), (10, 14), (15, 15)]
 
@@ -166,25 +167,32 @@ def tile_nonlocalmp_pa_t_kernel(tc, F, W1, b1, W2, b2, out):
         def emit_m(n):
             if n >= TILES:
                 return
-            h_tiles[n] = work.tile([P, COLS, PACK], BF16, name="hid", tag="hid", bufs=3, align_bytes=64)
             pq = p_tiles[n]
             nc.vector.tensor_tensor(out=pq[:, 0], in0=pq[:, 0], in1=pq[:, 1], op=ALU.max)
 
-        def emit_r(n):
+        def emit_pool(n, part):
             if n >= TILES:
                 return
-            nc.vector.tensor_copy(
-                out=h_tiles[n][:, 0 : COLS - GW, :].rearrange("p (c i) t -> p c t i", i=4),
-                in_=p_tiles[n][:, 0, :, 0 : COLS - GW].rearrange("p t (c i) -> p c t i", i=4),
+            if part == 0:
+                ht = work.tile([P, HALF, PACK], BF16, name="hida", tag="hida", bufs=3, align_bytes=64)
+            else:
+                ht = work.tile([P, HALF, PACK], BF16, name="hidb", tag="hidb", bufs=1, align_bytes=64)
+            h_tiles[(n, part)] = ht
+            lo = part * HALF + VS
+            hi = (part + 1) * HALF
+            nc.gpsimd.tensor_scalar(
+                out=ht[:, VS:HALF, :],
+                in0=p_tiles[n][:, 0, :, lo:hi].rearrange("p t w -> p w t"),
+                scalar1=1.0, scalar2=0.0, op0=ALU.mult, op1=ALU.add,
             )
 
-        def emit_rg(n):
-            if n >= TILES or GW == 0:
+        def emit_r(n, part):
+            if n >= TILES:
                 return
-            nc.gpsimd.tensor_scalar(
-                out=h_tiles[n][:, COLS - GW : COLS, :],
-                in0=p_tiles[n][:, 0, :, COLS - GW : COLS].rearrange("p t w -> p w t"),
-                scalar1=1.0, scalar2=0.0, op0=ALU.mult, op1=ALU.add,
+            lo = part * HALF
+            nc.vector.tensor_copy(
+                out=h_tiles[(n, part)][:, 0:VS, :].rearrange("p (c i) t -> p c t i", i=4),
+                in_=p_tiles[n][:, 0, :, lo : lo + VS].rearrange("p t (c i) -> p c t i", i=4),
             )
 
         def emit_q(n):
@@ -193,9 +201,12 @@ def tile_nonlocalmp_pa_t_kernel(tc, F, W1, b1, W2, b2, out):
             hc = const.tile([P, COLS], U32, name="hc%d" % n, tag="hc%d" % n, align_bytes=64)
             hs = const.tile([P, COLS], U8, name="hs%d" % n, tag="hs%d" % n, align_bytes=64)
             code_tiles[n] = (hc, hs)
-            nc.vector.quantize_mx(
-                out=hc[:].bitcast(FP8X4), scales=hs[:], in_=h_tiles[n][:].rearrange("p w t -> p (w t)")
-            )
+            for part in range(2):
+                cols = slice(part * HALF, (part + 1) * HALF)
+                nc.vector.quantize_mx(
+                    out=hc[:, cols].bitcast(FP8X4), scales=hs[:, cols],
+                    in_=h_tiles[(n, part)][:].rearrange("p w t -> p (w t)"),
+                )
 
         def emit_x(n, m):
             hc, hs = code_tiles[n]
@@ -271,7 +282,7 @@ def tile_nonlocalmp_pa_t_kernel(tc, F, W1, b1, W2, b2, out):
         for n in range(-2, TILES):
             live = n >= 0
             emit_m(n + 2)
-            emit_rg(n + 2)
+            emit_pool(n + 2, 0)
             if live:
                 x0 = emit_x(n, 0)
                 x1 = emit_x(n, 1)
@@ -281,10 +292,11 @@ def tile_nonlocalmp_pa_t_kernel(tc, F, W1, b1, W2, b2, out):
                 emit_l(n, 0)
                 x2 = emit_x(n, 2)
                 emit_g(n, 1, x1)
-            emit_r(n + 2)
+            emit_r(n + 2, 0)
             if n == -2:
                 nc.vector.quantize_mx(out=fc[:, 1024:2048].bitcast(FP8X4), scales=fs[:, 1024:2048], in_=f_bf)
             emit_q(n + 1)
+            emit_pool(n + 2, 1)
             emit_v(n + AHEAD, 1)
             if live:
                 x3 = emit_x(n, 3)
@@ -300,6 +312,7 @@ def tile_nonlocalmp_pa_t_kernel(tc, F, W1, b1, W2, b2, out):
             emit_v(n + AHEAD, 3)
             if live:
                 emit_g(n, 3, x3)
+            emit_r(n + 2, 1)
             if n == NODES - 1:
                 emit_tmp(0, [0, 1, 2])
             if n == NODES + 7:

@@ -32,7 +32,6 @@ LATE = [(0, 4), (5, 9), (10, 14), (15, 15)]
 def tile_nonlocalmp_pa_t_kernel(tc, F, W1, b1, W2, b2, out):
     nc = tc.nc
     with ExitStack() as ctx:
-        ctx.enter_context(tc.manual_schedule())
         const = ctx.enter_context(tc.tile_pool(name="const", bufs=1))
         work = ctx.enter_context(tc.tile_pool(name="work", bufs=2))
         psum = ctx.enter_context(tc.psum_pool(name="psum", bufs=2))

@@ -18,23 +18,27 @@ SETS = 64
 NODES = 16
 C = 512
 PACK = 4
-CHUNKS = 4
+CHUNKS = C // P
 WIN = 8
 COLS = WIN * SETS
-TILES = 32
+TILES = 2 * NODES
+HALF = COLS // 2
 SLOPE = 0.2
-VS = 96
-HALF = 256
+
 AHEAD = 4
+VS = 96
+V_BANKS = 3
+X_BANKS = 2
 LATE = [(0, 4), (5, 9), (10, 14), (15, 15)]
 
 
 def tile_nonlocalmp_pa_t_kernel(tc, F, W1, b1, W2, b2, out):
     nc = tc.nc
     with ExitStack() as ctx:
+        ctx.enter_context(tc.manual_schedule())
         const = ctx.enter_context(tc.tile_pool(name="const", bufs=1))
         work = ctx.enter_context(tc.tile_pool(name="work", bufs=2))
-        psum = ctx.enter_context(tc.psum_pool(name="psum", bufs=2))
+        psum = ctx.enter_context(tc.psum_pool(name="psum", bufs=X_BANKS))
 
         b1r = const.tile([P, CHUNKS], BF16, name="b1r", tag="b1r")
         b2r = const.tile([P, CHUNKS], BF16, name="b2r", tag="b2r")
@@ -63,16 +67,17 @@ def tile_nonlocalmp_pa_t_kernel(tc, F, W1, b1, W2, b2, out):
         fc = const.tile([P, 2 * NODES * SETS], U32, name="fc", tag="fc", align_bytes=64)
         fs = const.tile([P, 2 * NODES * SETS], U8, name="fs", tag="fs", align_bytes=64)
         for gg in range(4):
-            xt = psum.tile([P, 2, 2, P], F32, name="xt", tag="v", bufs=3)
+            xt = psum.tile([P, 2, 2, P], F32, name="xt", tag="v", bufs=V_BANKS)
             for gp in range(2):
                 words = f_raw[:, 2 * gg + gp, :].bitcast(F32)
                 for u in range(2):
                     nc.tensor.transpose(
                         out=xt[:, u, gp, :], in_=words[:, P * u : P * u + P], identity=ident[:]
                     )
-            dst = f_grp[:, :, 16 * gg : 16 * gg + 16, :]
-            src = xt[:].rearrange("p u g (b i) -> p i (g b) u", i=NODES)
-            nc.scalar.copy(out=dst, in_=src)
+            nc.scalar.copy(
+                out=f_grp[:, :, 16 * gg : 16 * gg + 16, :],
+                in_=xt[:].rearrange("p u g (b i) -> p i (g b) u", i=NODES),
+            )
 
         w1_grp = const.tile([P, 2, CHUNKS, P, PACK], BF16, name="w1_grp", tag="w1_grp", align_bytes=64)
         w1c = const.tile([P, 2 * C], U32, name="w1c", tag="w1c", align_bytes=64)
@@ -80,15 +85,11 @@ def tile_nonlocalmp_pa_t_kernel(tc, F, W1, b1, W2, b2, out):
         w2_grp = const.tile([P, CHUNKS, P, PACK], BF16, name="w2_grp", tag="w2_grp", align_bytes=64)
         w2c = const.tile([P, C], U32, name="w2c", tag="w2c", align_bytes=64)
         w2s = const.tile([P, C], U8, name="w2s", tag="w2s", align_bytes=64)
-
-        nc.vector.tensor_copy(
-            out=w1_grp[:, 0].rearrange("p o m t -> p m t o"),
-            in_=w1_raw[:, 0].rearrange("p t (m o) -> p m t o", o=CHUNKS),
-        )
-        nc.vector.tensor_copy(
-            out=w1_grp[:, 1].rearrange("p o m t -> p m t o"),
-            in_=w1_raw[:, 1].rearrange("p t (m o) -> p m t o", o=CHUNKS),
-        )
+        for a in range(2):
+            nc.vector.tensor_copy(
+                out=w1_grp[:, a].rearrange("p o m t -> p m t o"),
+                in_=w1_raw[:, a].rearrange("p t (m o) -> p m t o", o=CHUNKS),
+            )
         for a in range(2):
             nc.vector.quantize_mx(
                 out=w1c[:, a * C : (a + 1) * C].bitcast(FP8X4),
@@ -104,6 +105,7 @@ def tile_nonlocalmp_pa_t_kernel(tc, F, W1, b1, W2, b2, out):
         nc.vector.tensor_scalar(out=b2x[:], in0=b2r[:], scalar1=20.0, scalar2=None, op0=ALU.mult)
         b1s = const.tile([P, CHUNKS], F32, name="b1s", tag="b1s")
         nc.vector.tensor_scalar(out=b1s[:], in0=b1r[:], scalar1=SLOPE, scalar2=None, op0=ALU.mult)
+
         f_bf = f_grp[:].rearrange("p i b u -> p (i b u)").bitcast(BF16)
         for hf in range(2):
             nc.vector.quantize_mx(
@@ -116,9 +118,13 @@ def tile_nonlocalmp_pa_t_kernel(tc, F, W1, b1, W2, b2, out):
             [const.tile([P, COLS], F32, name="acc%d%d" % (h, m), tag="acc%d%d" % (h, m)) for m in range(CHUNKS)]
             for h in range(2)
         ]
-        tmp = acc
 
-        def mx(dst, lw, ls, rw, rs, start, stop):
+        pq_tiles = {}
+        hid_tiles = {}
+        code_tiles = {}
+        lin = {}
+
+        def mx_pass(dst, lw, ls, rw, rs, start, stop):
             nc.tensor.matmul_mx(
                 out=dst,
                 lhsT=lw.bitcast(FP8X4),
@@ -129,214 +135,202 @@ def tile_nonlocalmp_pa_t_kernel(tc, F, W1, b1, W2, b2, out):
                 stop=stop,
             )
 
-        p_tiles = {}
-        h_tiles = {}
-        code_tiles = {}
-        lin = {}
-
-        def emit_v(n, t):
+        def pair_sums(n, t):
             if n >= TILES:
                 return
             if t == 0:
-                p_tiles[n] = work.tile([P, 2, CHUNKS, COLS], BF16, name="pre", tag="pre", bufs=5)
-            r0 = WIN * (n // NODES)
-            a0 = SETS * r0
-            b0 = SETS * (r0 + n % NODES)
-            vt = psum.tile([P, COLS], F32, name="vt", tag="v", bufs=3)
+                pq_tiles[n] = work.tile([P, 2, CHUNKS, COLS], BF16, name="pre", tag="pre", bufs=AHEAD + 1)
+            first_node = WIN * (n // NODES)
+            a0 = SETS * first_node
+            b0 = SETS * (first_node + n % NODES)
+            vt = psum.tile([P, COLS], F32, name="vt", tag="v", bufs=V_BANKS)
             wa = slice(t * P, (t + 1) * P)
             wb = slice(C + t * P, C + (t + 1) * P)
-            mx(vt[:], w1c[:, wa], w1s[:, wa], fc[:, a0 : a0 + COLS], fs[:, a0 : a0 + COLS], True, False)
-            mx(vt[:], w1c[:, wb], w1s[:, wb], fc[:, b0 : b0 + COLS], fs[:, b0 : b0 + COLS], False, True)
+            mx_pass(vt[:], w1c[:, wa], w1s[:, wa], fc[:, a0 : a0 + COLS], fs[:, a0 : a0 + COLS], True, False)
+            mx_pass(vt[:], w1c[:, wb], w1s[:, wb], fc[:, b0 : b0 + COLS], fs[:, b0 : b0 + COLS], False, True)
+            p_out = pq_tiles[n][:, 0, t, :]
+            q_out = pq_tiles[n][:, 1, t, :]
             if n < 2 and t % 2 == 1:
+                nc.vector.tensor_scalar(out=p_out, in0=vt[:], scalar1=b1f[:, t : t + 1], scalar2=None, op0=ALU.add)
                 nc.vector.tensor_scalar(
-                    out=p_tiles[n][:, 0, t, :], in0=vt[:], scalar1=b1f[:, t : t + 1], scalar2=None, op0=ALU.add
-                )
-                nc.vector.tensor_scalar(
-                    out=p_tiles[n][:, 1, t, :], in0=vt[:], scalar1=b1f[:, t : t + 1], scalar2=SLOPE,
-                    op0=ALU.add, op1=ALU.mult,
+                    out=q_out, in0=vt[:], scalar1=b1f[:, t : t + 1], scalar2=SLOPE, op0=ALU.add, op1=ALU.mult
                 )
             else:
-                nc.scalar.activation(
-                    out=p_tiles[n][:, 0, t, :], in_=vt[:], func=ACT.Identity, bias=b1f[:, t : t + 1], scale=1.0
-                )
-                nc.scalar.activation(
-                    out=p_tiles[n][:, 1, t, :], in_=vt[:], func=ACT.Identity, bias=b1s[:, t : t + 1], scale=SLOPE
-                )
+                nc.scalar.activation(out=p_out, in_=vt[:], func=ACT.Identity, bias=b1f[:, t : t + 1], scale=1.0)
+                nc.scalar.activation(out=q_out, in_=vt[:], func=ACT.Identity, bias=b1s[:, t : t + 1], scale=SLOPE)
 
-        def emit_m(n):
+        def leaky_max(n):
             if n >= TILES:
                 return
-            pq = p_tiles[n]
+            pq = pq_tiles[n]
             nc.vector.tensor_tensor(out=pq[:, 0], in0=pq[:, 0], in1=pq[:, 1], op=ALU.max)
 
-        def emit_pool(n, part):
+        def regroup_gpsimd(n, part):
             if n >= TILES:
                 return
             if part == 0:
                 ht = work.tile([P, HALF, PACK], BF16, name="hida", tag="hida", bufs=3, align_bytes=64)
             else:
                 ht = work.tile([P, HALF, PACK], BF16, name="hidb", tag="hidb", bufs=1, align_bytes=64)
-            h_tiles[(n, part)] = ht
+            hid_tiles[(n, part)] = ht
             lo = part * HALF + VS
             hi = (part + 1) * HALF
             nc.gpsimd.tensor_scalar(
                 out=ht[:, VS:HALF, :],
-                in0=p_tiles[n][:, 0, :, lo:hi].rearrange("p t w -> p w t"),
-                scalar1=1.0, scalar2=0.0, op0=ALU.mult, op1=ALU.add,
+                in0=pq_tiles[n][:, 0, :, lo:hi].rearrange("p t w -> p w t"),
+                scalar1=1.0,
+                scalar2=0.0,
+                op0=ALU.mult,
+                op1=ALU.add,
             )
 
-        def emit_r(n, part):
+        def regroup_vector(n, part):
             if n >= TILES:
                 return
             lo = part * HALF
             nc.vector.tensor_copy(
-                out=h_tiles[(n, part)][:, 0:VS, :].rearrange("p (c i) t -> p c t i", i=4),
-                in_=p_tiles[n][:, 0, :, lo : lo + VS].rearrange("p t (c i) -> p c t i", i=4),
+                out=hid_tiles[(n, part)][:, 0:VS, :].rearrange("p (c i) t -> p c t i", i=4),
+                in_=pq_tiles[n][:, 0, :, lo : lo + VS].rearrange("p t (c i) -> p c t i", i=4),
             )
 
-        def emit_q(n):
+        def quantise_hidden(n):
             if n >= TILES or n < 0:
                 return
             hc = const.tile([P, COLS], U32, name="hc%d" % n, tag="hc%d" % n, align_bytes=64)
             hs = const.tile([P, COLS], U8, name="hs%d" % n, tag="hs%d" % n, align_bytes=64)
             code_tiles[n] = (hc, hs)
-            for part in range(2):
+            for part in (1, 0):
                 cols = slice(part * HALF, (part + 1) * HALF)
                 nc.vector.quantize_mx(
-                    out=hc[:, cols].bitcast(FP8X4), scales=hs[:, cols],
-                    in_=h_tiles[(n, part)][:].rearrange("p w t -> p (w t)"),
+                    out=hc[:, cols].bitcast(FP8X4),
+                    scales=hs[:, cols],
+                    in_=hid_tiles[(n, part)][:].rearrange("p w t -> p (w t)"),
                 )
 
-        def emit_x(n, m):
+        def second_matmul(n, m):
             hc, hs = code_tiles[n]
-            xt2 = psum.tile([P, COLS], F32, name="xs", tag="x")
+            xs = psum.tile([P, COLS], F32, name="xs", tag="x")
             wm = slice(m * P, (m + 1) * P)
-            mx(xt2[:], w2c[:, wm], w2s[:, wm], hc[:], hs[:], True, True)
-            return xt2
+            mx_pass(xs[:], w2c[:, wm], w2s[:, wm], hc[:], hs[:], True, True)
+            return xs
 
-        def emit_l(n, m):
+        def linear_pass(n, m, tag, bufs):
             hc, hs = code_tiles[n]
             s = n % NODES
             if s == 0:
-                lin[m] = psum.tile([P, COLS], F32, name="lin%d" % m, tag="lin%d" % m, bufs=1)
+                lin[m] = psum.tile([P, COLS], F32, name="lin%d" % m, tag=tag, bufs=bufs)
             wm = slice(m * P, (m + 1) * P)
-            mx(lin[m][:], w2c[:, wm], w2s[:, wm], hc[:], hs[:], s == 0, s == NODES - 1)
+            mx_pass(lin[m][:], w2c[:, wm], w2s[:, wm], hc[:], hs[:], s == 0, s == NODES - 1)
 
-        def emit_late(h, first, last):
-            m = CHUNKS - 1
-            wm = slice(m * P, (m + 1) * P)
-            for n in range(NODES * h + first, NODES * h + last + 1):
-                s = n % NODES
-                if s == 0:
-                    lin[m] = psum.tile([P, COLS], F32, name="lin3", tag="v", bufs=3)
-                hc, hs = code_tiles[n]
-                mx(lin[m][:], w2c[:, wm], w2s[:, wm], hc[:], hs[:], s == 0, s == NODES - 1)
+        def linear_now(n, m):
+            linear_pass(n, m, "lin%d" % m, 1)
 
-        def emit_g(n, m, xt2):
+        def linear_late(h, first, last):
+            for s in range(first, last + 1):
+                linear_pass(NODES * h + s, CHUNKS - 1, "v", V_BANKS)
+
+        def relu_sum(n, m, xs):
             a = acc[n // NODES][m]
             if n % NODES == 0:
                 nc.vector.tensor_scalar(
-                    out=a[:], in0=xt2[:], scalar1=nb2[:, m : m + 1], scalar2=b2x[:, m : m + 1],
+                    out=a[:], in0=xs[:], scalar1=nb2[:, m : m + 1], scalar2=b2x[:, m : m + 1],
                     op0=ALU.max, op1=ALU.add,
                 )
             else:
                 nc.vector.scalar_tensor_tensor(
-                    out=a[:], in0=xt2[:], scalar=nb2[:, m : m + 1], in1=a[:], op0=ALU.max, op1=ALU.add
+                    out=a[:], in0=xs[:], scalar=nb2[:, m : m + 1], in1=a[:], op0=ALU.max, op1=ALU.add
                 )
 
-        def emit_tmp(h, chunks):
-            for m in chunks:
-                nc.vector.scalar_tensor_tensor(
-                    out=tmp[h][m][:], in0=lin[m][:], scalar=0.25, in1=acc[h][m][:], op0=ALU.mult, op1=ALU.add
-                )
+        def join_sums(h, m):
+            nc.vector.scalar_tensor_tensor(
+                out=acc[h][m][:], in0=lin[m][:], scalar=0.25, in1=acc[h][m][:], op0=ALU.mult, op1=ALU.add
+            )
 
-        def emit_out(h, q, tag, on_vector):
-            tp = psum.tile([P, CHUNKS, P], F32, name="tp", tag=tag, bufs=(3 if tag == "v" else 2))
-            for m in range(CHUNKS):
-                nc.tensor.transpose(out=tp[:, m, :], in_=tmp[h][m][:, q * P : (q + 1) * P], identity=ident[:])
+        def transpose_block(tp, h, m, q):
+            nc.tensor.transpose(out=tp[:, m, :], in_=acc[h][m][:, q * P : (q + 1) * P], identity=ident[:])
+
+        def store_block(tp, h, q, on_vector, second_queue):
             res = work.tile([P, P, CHUNKS], F32, name="res", tag="res", bufs=4)
             src = tp[:].rearrange("p m c -> p c m")
             if on_vector:
                 nc.vector.tensor_scalar(out=res[:], in0=src, scalar1=0.8, scalar2=None, op0=ALU.mult)
             else:
                 nc.scalar.mul(out=res[:], in_=src, mul=0.8)
+            queues = [nc.sync, second_queue]
             for k in range(2):
-                node = WIN * h + 2 * q + k
-                nc.sync.dma_start(
-                    out=out[:, node, :], in_=res[k * SETS : (k + 1) * SETS].rearrange("p c m -> p (c m)")
+                queues[k].dma_start(
+                    out=out[:, WIN * h + 2 * q + k, :],
+                    in_=res[k * SETS : (k + 1) * SETS].rearrange("p c m -> p (c m)"),
                 )
 
         for t in range(CHUNKS):
-            emit_v(0, t)
+            pair_sums(0, t)
         nc.vector.tensor_copy(
             out=w2_grp[:].rearrange("p o m t -> p m t o"),
             in_=w2_raw[:].rearrange("p t (m o) -> p m t o", o=CHUNKS),
         )
         for t in range(CHUNKS):
-            emit_v(1, t)
+            pair_sums(1, t)
         nc.vector.quantize_mx(
             out=w2c[:].bitcast(FP8X4), scales=w2s[:], in_=w2_grp[:].rearrange("p o m t -> p (o m t)")
         )
 
+        leaky_max(0)
         for n in range(-2, TILES):
             live = n >= 0
-            emit_m(n + 2)
-            emit_pool(n + 2, 0)
+            regroup_gpsimd(n + 2, 0)
             if live:
-                x0 = emit_x(n, 0)
-                x1 = emit_x(n, 1)
-            emit_v(n + AHEAD, 0)
+                x0 = second_matmul(n, 0)
+                x1 = second_matmul(n, 1)
+            pair_sums(n + AHEAD, 0)
             if live:
-                emit_g(n, 0, x0)
-                emit_l(n, 0)
-                x2 = emit_x(n, 2)
-                emit_g(n, 1, x1)
-            emit_r(n + 2, 0)
+                relu_sum(n, 0, x0)
+                linear_now(n, 0)
+                x2 = second_matmul(n, 2)
+                relu_sum(n, 1, x1)
+            regroup_vector(n + 2, 0)
             if n == -2:
                 nc.vector.quantize_mx(out=fc[:, 1024:2048].bitcast(FP8X4), scales=fs[:, 1024:2048], in_=f_bf)
-            emit_q(n + 1)
-            emit_pool(n + 2, 1)
-            emit_v(n + AHEAD, 1)
+            quantise_hidden(n + 1)
+            regroup_gpsimd(n + 2, 1)
+            pair_sums(n + AHEAD, 1)
             if live:
-                x3 = emit_x(n, 3)
-                emit_g(n, 2, x2)
-                emit_l(n, 1)
-            emit_v(n + AHEAD, 2)
+                x3 = second_matmul(n, 3)
+                relu_sum(n, 2, x2)
+                linear_now(n, 1)
+            pair_sums(n + AHEAD, 2)
             if live:
-                emit_l(n, 2)
+                linear_now(n, 2)
             if NODES <= n < NODES + 8:
-                emit_late(0, 2 * (n - NODES), 2 * (n - NODES) + 1)
+                linear_late(0, 2 * (n - NODES), 2 * (n - NODES) + 1)
             if n >= TILES - 4:
-                emit_late(1, LATE[n - TILES + 4][0], LATE[n - TILES + 4][1])
-            emit_v(n + AHEAD, 3)
+                linear_late(1, LATE[n - TILES + 4][0], LATE[n - TILES + 4][1])
+            pair_sums(n + AHEAD, 3)
             if live:
-                emit_g(n, 3, x3)
-            emit_r(n + 2, 1)
+                relu_sum(n, 3, x3)
+            leaky_max(n + 3)
+            regroup_vector(n + 2, 1)
             if n == NODES - 1:
-                emit_tmp(0, [0, 1, 2])
+                for m in range(CHUNKS - 1):
+                    join_sums(0, m)
             if n == NODES + 7:
-                emit_tmp(0, [3])
+                join_sums(0, CHUNKS - 1)
             if NODES + 8 <= n < NODES + 12:
-                emit_out(0, n - NODES - 8, "v", False)
+                q = n - NODES - 8
+                tp = psum.tile([P, CHUNKS, P], F32, name="tp", tag="v", bufs=V_BANKS)
+                for m in range(CHUNKS):
+                    transpose_block(tp, 0, m, q)
+                store_block(tp, 0, q, False, nc.sync)
 
         tps = []
         for q in range(4):
-            tag = "v" if q < 2 else "x"
-            tps.append(psum.tile([P, CHUNKS, P], F32, name="tq%d" % q, tag=tag, bufs=(3 if tag == "v" else 2)))
-        for m in range(CHUNKS):
-            emit_tmp(1, [m])
-            for q in range(4):
-                nc.tensor.transpose(out=tps[q][:, m, :], in_=tmp[1][m][:, q * P : (q + 1) * P], identity=ident[:])
-        for q in range(4):
-            res = work.tile([P, P, CHUNKS], F32, name="res", tag="res", bufs=4)
-            src = tps[q][:].rearrange("p m c -> p c m")
-            if q % 2 == 1:
-                nc.vector.tensor_scalar(out=res[:], in0=src, scalar1=0.8, scalar2=None, op0=ALU.mult)
+            if q < 2:
+                tps.append(psum.tile([P, CHUNKS, P], F32, name="tq%d" % q, tag="v", bufs=V_BANKS))
             else:
-                nc.scalar.mul(out=res[:], in_=src, mul=0.8)
-            for k in range(2):
-                node = WIN + 2 * q + k
-                eng = nc.sync if k == 0 else nc.scalar
-                eng.dma_start(
-                    out=out[:, node, :], in_=res[k * SETS : (k + 1) * SETS].rearrange("p c m -> p (c m)")
-                )
+                tps.append(psum.tile([P, CHUNKS, P], F32, name="tq%d" % q, tag="x", bufs=X_BANKS))
+        for m in range(CHUNKS):
+            join_sums(1, m)
+            for q in range(4):
+                transpose_block(tps[q], 1, m, q)
+        for q in range(4):
+            store_block(tps[q], 1, q, q % 2 == 1, nc.scalar)

from contextlib import ExitStack

import concourse.mybir as mybir
from concourse.masks import make_identity

FLOPS = 2 * 1024 * 1024 * 512 + 2 * 16384 * 512 * 512

F32 = mybir.dt.float32
BF16 = mybir.dt.bfloat16
U32 = mybir.dt.uint32
U8 = mybir.dt.uint8
FP8X4 = mybir.dt.float8_e4m3fn_x4
ALU = mybir.AluOpType
ACT = mybir.ActivationFunctionType

P = 128
SETS = 64
NODES = 16
C = 512
PACK = 4
CHUNKS = C // P
WIN = 8
COLS = WIN * SETS
TILES = 2 * NODES
HALF = COLS // 2
SLOPE = 0.2

AHEAD = 4
VS = 96
V_BANKS = 3
X_BANKS = 2
LATE = [(0, 4), (5, 9), (10, 14), (15, 15)]


def tile_nonlocalmp_pa_t_kernel(tc, F, W1, b1, W2, b2, out):
    nc = tc.nc
    with ExitStack() as ctx:
        ctx.enter_context(tc.manual_schedule())
        const = ctx.enter_context(tc.tile_pool(name="const", bufs=1))
        work = ctx.enter_context(tc.tile_pool(name="work", bufs=2))
        psum = ctx.enter_context(tc.psum_pool(name="psum", bufs=X_BANKS))

        b1r = const.tile([P, CHUNKS], BF16, name="b1r", tag="b1r")
        b2r = const.tile([P, CHUNKS], BF16, name="b2r", tag="b2r")
        nc.scalar.dma_start(out=b1r[:], in_=b1.rearrange("(p t) -> p t", t=CHUNKS))
        nc.scalar.dma_start(out=b2r[:], in_=b2.rearrange("(p t) -> p t", t=CHUNKS))

        w1_raw = const.tile([P, 2, PACK, C], BF16, name="w1_raw", tag="w1_raw")
        for a in range(2):
            for u in range(2):
                r = a * C + u * 256
                nc.sync.dma_start(
                    out=w1_raw[:, a, 2 * u : 2 * u + 2, :],
                    in_=W1[r : r + 256, :].rearrange("(p e) c -> p e c", e=2),
                )
        f_raw = const.tile([P, 8, C], BF16, name="f_raw", tag="f_raw")
        f_rows = F.rearrange("b i c -> (b i) c").rearrange("(g p) c -> p g c", p=P)
        nc.sync.dma_start(out=f_raw[:, 0:4, :], in_=f_rows[:, 0:4, :])
        nc.sync.dma_start(out=f_raw[:, 4:8, :], in_=f_rows[:, 4:8, :])
        w2_raw = const.tile([P, PACK, C], BF16, name="w2_raw", tag="w2_raw")
        nc.sync.dma_start(out=w2_raw[:], in_=W2.rearrange("(p t) n -> p t n", t=PACK))

        ident = const.tile([P, P], F32, name="ident", tag="ident")
        make_identity(nc, ident[:])

        f_grp = const.tile([P, NODES, SETS, 2], F32, name="f_grp", tag="f_grp", align_bytes=64)
        fc = const.tile([P, 2 * NODES * SETS], U32, name="fc", tag="fc", align_bytes=64)
        fs = const.tile([P, 2 * NODES * SETS], U8, name="fs", tag="fs", align_bytes=64)
        for gg in range(4):
            xt = psum.tile([P, 2, 2, P], F32, name="xt", tag="v", bufs=V_BANKS)
            for gp in range(2):
                words = f_raw[:, 2 * gg + gp, :].bitcast(F32)
                for u in range(2):
                    nc.tensor.transpose(
                        out=xt[:, u, gp, :], in_=words[:, P * u : P * u + P], identity=ident[:]
                    )
            nc.scalar.copy(
                out=f_grp[:, :, 16 * gg : 16 * gg + 16, :],
                in_=xt[:].rearrange("p u g (b i) -> p i (g b) u", i=NODES),
            )

        w1_grp = const.tile([P, 2, CHUNKS, P, PACK], BF16, name="w1_grp", tag="w1_grp", align_bytes=64)
        w1c = const.tile([P, 2 * C], U32, name="w1c", tag="w1c", align_bytes=64)
        w1s = const.tile([P, 2 * C], U8, name="w1s", tag="w1s", align_bytes=64)
        w2_grp = const.tile([P, CHUNKS, P, PACK], BF16, name="w2_grp", tag="w2_grp", align_bytes=64)
        w2c = const.tile([P, C], U32, name="w2c", tag="w2c", align_bytes=64)
        w2s = const.tile([P, C], U8, name="w2s", tag="w2s", align_bytes=64)
        for a in range(2):
            nc.vector.tensor_copy(
                out=w1_grp[:, a].rearrange("p o m t -> p m t o"),
                in_=w1_raw[:, a].rearrange("p t (m o) -> p m t o", o=CHUNKS),
            )
        for a in range(2):
            nc.vector.quantize_mx(
                out=w1c[:, a * C : (a + 1) * C].bitcast(FP8X4),
                scales=w1s[:, a * C : (a + 1) * C],
                in_=w1_grp[:, a].rearrange("p o m t -> p (o m t)"),
            )

        b1f = const.tile([P, CHUNKS], F32, name="b1f", tag="b1f")
        nb2 = const.tile([P, CHUNKS], F32, name="nb2", tag="nb2")
        b2x = const.tile([P, CHUNKS], F32, name="b2x", tag="b2x")
        nc.vector.tensor_copy(out=b1f[:], in_=b1r[:])
        nc.vector.tensor_scalar(out=nb2[:], in0=b2r[:], scalar1=-1.0, scalar2=None, op0=ALU.mult)
        nc.vector.tensor_scalar(out=b2x[:], in0=b2r[:], scalar1=20.0, scalar2=None, op0=ALU.mult)
        b1s = const.tile([P, CHUNKS], F32, name="b1s", tag="b1s")
        nc.vector.tensor_scalar(out=b1s[:], in0=b1r[:], scalar1=SLOPE, scalar2=None, op0=ALU.mult)

        f_bf = f_grp[:].rearrange("p i b u -> p (i b u)").bitcast(BF16)
        for hf in range(2):
            nc.vector.quantize_mx(
                out=fc[:, hf * COLS : (hf + 1) * COLS].bitcast(FP8X4),
                scales=fs[:, hf * COLS : (hf + 1) * COLS],
                in_=f_bf[:, hf * COLS * PACK : (hf + 1) * COLS * PACK],
            )

        acc = [
            [const.tile([P, COLS], F32, name="acc%d%d" % (h, m), tag="acc%d%d" % (h, m)) for m in range(CHUNKS)]
            for h in range(2)
        ]

        pq_tiles = {}
        hid_tiles = {}
        code_tiles = {}
        lin = {}

        def mx_pass(dst, lw, ls, rw, rs, start, stop):
            nc.tensor.matmul_mx(
                out=dst,
                lhsT=lw.bitcast(FP8X4),
                lhsT_scale=ls,
                rhs=rw.bitcast(FP8X4),
                rhs_scale=rs,
                start=start,
                stop=stop,
            )

        def pair_sums(n, t):
            if n >= TILES:
                return
            if t == 0:
                pq_tiles[n] = work.tile([P, 2, CHUNKS, COLS], BF16, name="pre", tag="pre", bufs=AHEAD + 1)
            first_node = WIN * (n // NODES)
            a0 = SETS * first_node
            b0 = SETS * (first_node + n % NODES)
            vt = psum.tile([P, COLS], F32, name="vt", tag="v", bufs=V_BANKS)
            wa = slice(t * P, (t + 1) * P)
            wb = slice(C + t * P, C + (t + 1) * P)
            mx_pass(vt[:], w1c[:, wa], w1s[:, wa], fc[:, a0 : a0 + COLS], fs[:, a0 : a0 + COLS], True, False)
            mx_pass(vt[:], w1c[:, wb], w1s[:, wb], fc[:, b0 : b0 + COLS], fs[:, b0 : b0 + COLS], False, True)
            p_out = pq_tiles[n][:, 0, t, :]
            q_out = pq_tiles[n][:, 1, t, :]
            if n < 2 and t % 2 == 1:
                nc.vector.tensor_scalar(out=p_out, in0=vt[:], scalar1=b1f[:, t : t + 1], scalar2=None, op0=ALU.add)
                nc.vector.tensor_scalar(
                    out=q_out, in0=vt[:], scalar1=b1f[:, t : t + 1], scalar2=SLOPE, op0=ALU.add, op1=ALU.mult
                )
            else:
                nc.scalar.activation(out=p_out, in_=vt[:], func=ACT.Identity, bias=b1f[:, t : t + 1], scale=1.0)
                nc.scalar.activation(out=q_out, in_=vt[:], func=ACT.Identity, bias=b1s[:, t : t + 1], scale=SLOPE)

        def leaky_max(n):
            if n >= TILES:
                return
            pq = pq_tiles[n]
            nc.vector.tensor_tensor(out=pq[:, 0], in0=pq[:, 0], in1=pq[:, 1], op=ALU.max)

        def regroup_gpsimd(n, part):
            if n >= TILES:
                return
            if part == 0:
                ht = work.tile([P, HALF, PACK], BF16, name="hida", tag="hida", bufs=3, align_bytes=64)
            else:
                ht = work.tile([P, HALF, PACK], BF16, name="hidb", tag="hidb", bufs=1, align_bytes=64)
            hid_tiles[(n, part)] = ht
            lo = part * HALF + VS
            hi = (part + 1) * HALF
            nc.gpsimd.tensor_scalar(
                out=ht[:, VS:HALF, :],
                in0=pq_tiles[n][:, 0, :, lo:hi].rearrange("p t w -> p w t"),
                scalar1=1.0,
                scalar2=0.0,
                op0=ALU.mult,
                op1=ALU.add,
            )

        def regroup_vector(n, part):
            if n >= TILES:
                return
            lo = part * HALF
            nc.vector.tensor_copy(
                out=hid_tiles[(n, part)][:, 0:VS, :].rearrange("p (c i) t -> p c t i", i=4),
                in_=pq_tiles[n][:, 0, :, lo : lo + VS].rearrange("p t (c i) -> p c t i", i=4),
            )

        def quantise_hidden(n):
            if n >= TILES or n < 0:
                return
            hc = const.tile([P, COLS], U32, name="hc%d" % n, tag="hc%d" % n, align_bytes=64)
            hs = const.tile([P, COLS], U8, name="hs%d" % n, tag="hs%d" % n, align_bytes=64)
            code_tiles[n] = (hc, hs)
            for part in (1, 0):
                cols = slice(part * HALF, (part + 1) * HALF)
                nc.vector.quantize_mx(
                    out=hc[:, cols].bitcast(FP8X4),
                    scales=hs[:, cols],
                    in_=hid_tiles[(n, part)][:].rearrange("p w t -> p (w t)"),
                )

        def second_matmul(n, m):
            hc, hs = code_tiles[n]
            xs = psum.tile([P, COLS], F32, name="xs", tag="x")
            wm = slice(m * P, (m + 1) * P)
            mx_pass(xs[:], w2c[:, wm], w2s[:, wm], hc[:], hs[:], True, True)
            return xs

        def linear_pass(n, m, tag, bufs):
            hc, hs = code_tiles[n]
            s = n % NODES
            if s == 0:
                lin[m] = psum.tile([P, COLS], F32, name="lin%d" % m, tag=tag, bufs=bufs)
            wm = slice(m * P, (m + 1) * P)
            mx_pass(lin[m][:], w2c[:, wm], w2s[:, wm], hc[:], hs[:], s == 0, s == NODES - 1)

        def linear_now(n, m):
            linear_pass(n, m, "lin%d" % m, 1)

        def linear_late(h, first, last):
            for s in range(first, last + 1):
                linear_pass(NODES * h + s, CHUNKS - 1, "v", V_BANKS)

        def relu_sum(n, m, xs):
            a = acc[n // NODES][m]
            if n % NODES == 0:
                nc.vector.tensor_scalar(
                    out=a[:], in0=xs[:], scalar1=nb2[:, m : m + 1], scalar2=b2x[:, m : m + 1],
                    op0=ALU.max, op1=ALU.add,
                )
            else:
                nc.vector.scalar_tensor_tensor(
                    out=a[:], in0=xs[:], scalar=nb2[:, m : m + 1], in1=a[:], op0=ALU.max, op1=ALU.add
                )

        def join_sums(h, m):
            nc.vector.scalar_tensor_tensor(
                out=acc[h][m][:], in0=lin[m][:], scalar=0.25, in1=acc[h][m][:], op0=ALU.mult, op1=ALU.add
            )

        def transpose_block(tp, h, m, q):
            nc.tensor.transpose(out=tp[:, m, :], in_=acc[h][m][:, q * P : (q + 1) * P], identity=ident[:])

        def store_block(tp, h, q, on_vector, second_queue):
            res = work.tile([P, P, CHUNKS], F32, name="res", tag="res", bufs=4)
            src = tp[:].rearrange("p m c -> p c m")
            if on_vector:
                nc.vector.tensor_scalar(out=res[:], in0=src, scalar1=0.8, scalar2=None, op0=ALU.mult)
            else:
                nc.scalar.mul(out=res[:], in_=src, mul=0.8)
            queues = [nc.sync, second_queue]
            for k in range(2):
                queues[k].dma_start(
                    out=out[:, WIN * h + 2 * q + k, :],
                    in_=res[k * SETS : (k + 1) * SETS].rearrange("p c m -> p (c m)"),
                )

        for t in range(CHUNKS):
            pair_sums(0, t)
        nc.vector.tensor_copy(
            out=w2_grp[:].rearrange("p o m t -> p m t o"),
            in_=w2_raw[:].rearrange("p t (m o) -> p m t o", o=CHUNKS),
        )
        for t in range(CHUNKS):
            pair_sums(1, t)
        nc.vector.quantize_mx(
            out=w2c[:].bitcast(FP8X4), scales=w2s[:], in_=w2_grp[:].rearrange("p o m t -> p (o m t)")
        )

        leaky_max(0)
        for n in range(-2, TILES):
            live = n >= 0
            regroup_gpsimd(n + 2, 0)
            if live:
                x0 = second_matmul(n, 0)
                x1 = second_matmul(n, 1)
            pair_sums(n + AHEAD, 0)
            if live:
                relu_sum(n, 0, x0)
                linear_now(n, 0)
                x2 = second_matmul(n, 2)
                relu_sum(n, 1, x1)
            regroup_vector(n + 2, 0)
            if n == -2:
                nc.vector.quantize_mx(out=fc[:, 1024:2048].bitcast(FP8X4), scales=fs[:, 1024:2048], in_=f_bf)
            quantise_hidden(n + 1)
            regroup_gpsimd(n + 2, 1)
            pair_sums(n + AHEAD, 1)
            if live:
                x3 = second_matmul(n, 3)
                relu_sum(n, 2, x2)
                linear_now(n, 1)
            pair_sums(n + AHEAD, 2)
            if live:
                linear_now(n, 2)
            if NODES <= n < NODES + 8:
                linear_late(0, 2 * (n - NODES), 2 * (n - NODES) + 1)
            if n >= TILES - 4:
                linear_late(1, LATE[n - TILES + 4][0], LATE[n - TILES + 4][1])
            pair_sums(n + AHEAD, 3)
            if live:
                relu_sum(n, 3, x3)
            leaky_max(n + 3)
            regroup_vector(n + 2, 1)
            if n == NODES - 1:
                for m in range(CHUNKS - 1):
                    join_sums(0, m)
            if n == NODES + 7:
                join_sums(0, CHUNKS - 1)
            if NODES + 8 <= n < NODES + 12:
                q = n - NODES - 8
                tp = psum.tile([P, CHUNKS, P], F32, name="tp", tag="v", bufs=V_BANKS)
                for m in range(CHUNKS):
                    transpose_block(tp, 0, m, q)
                store_block(tp, 0, q, False, nc.sync)

        tps = []
        for q in range(4):
            if q < 2:
                tps.append(psum.tile([P, CHUNKS, P], F32, name="tq%d" % q, tag="v", bufs=V_BANKS))
            else:
                tps.append(psum.tile([P, CHUNKS, P], F32, name="tq%d" % q, tag="x", bufs=X_BANKS))
        for m in range(CHUNKS):
            join_sums(1, m)
            for q in range(4):
                transpose_block(tps[q], 1, m, q)
        for q in range(4):
            store_block(tps[q], 1, q, q % 2 == 1, nc.scalar)
